import numpy as np
import ml_dtypes

BF16 = ml_dtypes.bfloat16


def bf(x):
    return np.asarray(x, np.float32).astype(BF16)


def f32(x):
    return np.asarray(x, np.float32)


def f64(x):
    return np.asarray(x).astype(np.float64)


def striped(idx):
    return np.tile(idx.reshape(-1, 16).T, (8, 1))


S, D, F, E, B, L, POOL, P, N = 2048, 128, 128, 128, 128, 32, 4, 8, 4096


def setup_inputs():
    return {"table": bf(np.random.standard_normal((D, S))), "w": bf(np.random.standard_normal((D, F)) / np.sqrt(D)), "w2": bf(np.random.standard_normal((F, E)) / np.sqrt(F)), "offs": striped(np.random.permutation(np.tile(np.arange(S), 2))[:N])}


def reference(table, w, w2, offs):
    idx = offs[:16].T.reshape(-1)
    scores = f64(w).T @ f64(table)[:, idx]
    h1 = np.maximum(scores.reshape(F, B, P, POOL).max(axis=3), 0.0)
    v = np.einsum('fe,fbp->ebp', f64(w2), h1)
    return v.mean(axis=2)

@@ -1,0 +1,79 @@
+import concourse.mybir as mybir
+
+BF16, F32, U16 = mybir.dt.bfloat16, mybir.dt.float32, mybir.dt.uint16
+
+FEATURES = 128
+VOCABULARY = 2048
+FILTERS = 128
+OUT_FEATURES = 128
+DESCRIPTIONS = 128
+POSITIONS = 8
+WINDOW = 4
+ENTRIES = DESCRIPTIONS * POSITIONS * WINDOW
+
+PIECE = 512
+PIECES = ENTRIES // PIECE
+PIECE_DESCRIPTIONS = PIECE // (POSITIONS * WINDOW)
+OFFSETS_IN_A_COLUMN = 16
+
+FLOPS = 2 * FEATURES * FILTERS * ENTRIES + 2 * FILTERS * OUT_FEATURES * DESCRIPTIONS
+
+
+def tile_dkrl_kernel(tc, table, w, w2, offs, out):
+    nc = tc.nc
+    with (
+        tc.tile_pool(name="held", bufs=1) as held,
+        tc.psum_pool(name="score_banks", bufs=4) as score_banks,
+        tc.psum_pool(name="out_bank", bufs=1) as out_bank,
+    ):
+        offsets = held.tile([128, ENTRIES // OFFSETS_IN_A_COLUMN], U16, name="offsets")
+        nc.sync.dma_start(offsets[:], offs)
+        words = held.tile([FEATURES, VOCABULARY], BF16, name="words")
+        nc.scalar.dma_start(words[:], table)
+        filters = held.tile([FEATURES, FILTERS], BF16, name="filters")
+        nc.sync.dma_start(filters[:], w)
+        second_layer = held.tile([FILTERS, OUT_FEATURES], BF16, name="second_layer")
+        nc.sync.dma_start(second_layer[:], w2)
+
+        pooled = held.tile([FILTERS, POSITIONS, DESCRIPTIONS], F32, name="pooled")
+        h1_eighth = held.tile([FILTERS, POSITIONS, DESCRIPTIONS], BF16, name="h1_eighth")
+
+        for piece in range(PIECES):
+            first_column = piece * PIECE // OFFSETS_IN_A_COLUMN
+            last_column = (piece + 1) * PIECE // OFFSETS_IN_A_COLUMN
+            first_b = piece * PIECE_DESCRIPTIONS
+            last_b = (piece + 1) * PIECE_DESCRIPTIONS
+
+            scores = score_banks.tile([FILTERS, PIECE], F32, name="scores")
+            nc.tensor.matmul(
+                scores[:],
+                filters[:],
+                words[:].indirect(offsets[:, first_column:last_column]),
+                start=True,
+                stop=True,
+            )
+            nc.vector.tensor_reduce(
+                pooled[:, :, first_b:last_b],
+                scores[:].rearrange("f (b p t) -> f p b t", p=POSITIONS, t=WINDOW),
+                mybir.AxisListType.X,
+                mybir.AluOpType.max,
+            )
+            nc.scalar.activation(
+                h1_eighth[:, :, first_b:last_b],
+                pooled[:, :, first_b:last_b],
+                mybir.ActivationFunctionType.Relu,
+                scale=1.0 / POSITIONS,
+            )
+
+        mean = out_bank.tile([OUT_FEATURES, DESCRIPTIONS], F32, name="mean")
+        for p in range(POSITIONS):
+            nc.tensor.matmul(
+                mean[:],
+                second_layer[:],
+                h1_eighth[:, p, :],
+                start=(p == 0),
+                stop=(p == POSITIONS - 1),
+            )
+        result = held.tile([OUT_FEATURES, DESCRIPTIONS], F32, name="result")
+        nc.vector.tensor_copy(result[:], mean[:])
+        nc.sync.dma_start(out, result[:])

@@ -16,6 +16,8 @@ PIECES = ENTRIES // PIECE
 PIECE_DESCRIPTIONS = PIECE // (POSITIONS * WINDOW)
 OFFSETS_IN_A_COLUMN = 16
 
+WARM_UP_MATMULS = 6
+
 FLOPS = 2 * FEATURES * FILTERS * ENTRIES + 2 * FILTERS * OUT_FEATURES * DESCRIPTIONS
 
 
@@ -25,6 +27,7 @@ def tile_dkrl_kernel(tc, table, w, w2, offs, out):
         tc.tile_pool(name="held", bufs=1) as held,
         tc.psum_pool(name="score_banks", bufs=4) as score_banks,
         tc.psum_pool(name="out_bank", bufs=1) as out_bank,
+        tc.psum_pool(name="idle_bank", bufs=1) as idle_bank,
     ):
         offsets = held.tile([128, ENTRIES // OFFSETS_IN_A_COLUMN], U16, name="offsets")
         nc.sync.dma_start(offsets[:], offs)
@@ -34,6 +37,12 @@ def tile_dkrl_kernel(tc, table, w, w2, offs, out):
         nc.sync.dma_start(filters[:], w)
         second_layer = held.tile([FILTERS, OUT_FEATURES], BF16, name="second_layer")
         nc.sync.dma_start(second_layer[:], w2)
+
+        zeros = held.tile([128, PIECE], BF16, name="zeros")
+        nc.vector.memset(zeros[:], 0.0)
+        unused = idle_bank.tile([128, PIECE], F32, name="unused")
+        for repeat in range(WARM_UP_MATMULS):
+            nc.tensor.matmul(unused[:], zeros[:, 0:128], zeros[:], start=True, stop=True)
 
         pooled = held.tile([FILTERS, POSITIONS, DESCRIPTIONS], F32, name="pooled")
         h1_eighth = held.tile([FILTERS, POSITIONS, DESCRIPTIONS], BF16, name="h1_eighth")

@@ -1,6 +1,8 @@
 import concourse.mybir as mybir
 
 BF16, F32, U16 = mybir.dt.bfloat16, mybir.dt.float32, mybir.dt.uint16
+MAX = mybir.AluOpType.max
+RELU = mybir.ActivationFunctionType.Relu
 
 FEATURES = 128
 VOCABULARY = 2048
@@ -16,8 +18,6 @@ PIECES = ENTRIES // PIECE
 PIECE_DESCRIPTIONS = PIECE // (POSITIONS * WINDOW)
 OFFSETS_IN_A_COLUMN = 16
 
-WARM_UP_MATMULS = 6
-
 FLOPS = 2 * FEATURES * FILTERS * ENTRIES + 2 * FILTERS * OUT_FEATURES * DESCRIPTIONS
 
 
@@ -25,9 +25,9 @@ def tile_dkrl_kernel(tc, table, w, w2, offs, out):
     nc = tc.nc
     with (
         tc.tile_pool(name="held", bufs=1) as held,
+        tc.tile_pool(name="work", bufs=3) as work,
         tc.psum_pool(name="score_banks", bufs=4) as score_banks,
         tc.psum_pool(name="out_bank", bufs=1) as out_bank,
-        tc.psum_pool(name="idle_bank", bufs=1) as idle_bank,
     ):
         offsets = held.tile([128, ENTRIES // OFFSETS_IN_A_COLUMN], U16, name="offsets")
         nc.sync.dma_start(offsets[:], offs)
@@ -38,14 +38,7 @@ def tile_dkrl_kernel(tc, table, w, w2, offs, out):
         second_layer = held.tile([FILTERS, OUT_FEATURES], BF16, name="second_layer")
         nc.sync.dma_start(second_layer[:], w2)
 
-        zeros = held.tile([128, PIECE], BF16, name="zeros")
-        nc.vector.memset(zeros[:], 0.0)
-        unused = idle_bank.tile([128, PIECE], F32, name="unused")
-        for repeat in range(WARM_UP_MATMULS):
-            nc.tensor.matmul(unused[:], zeros[:, 0:128], zeros[:], start=True, stop=True)
-
-        pooled = held.tile([FILTERS, POSITIONS, DESCRIPTIONS], F32, name="pooled")
-        h1_eighth = held.tile([FILTERS, POSITIONS, DESCRIPTIONS], BF16, name="h1_eighth")
+        h1 = held.tile([FILTERS, POSITIONS, DESCRIPTIONS], BF16, name="h1")
 
         for piece in range(PIECES):
             first_column = piece * PIECE // OFFSETS_IN_A_COLUMN
@@ -61,28 +54,30 @@ def tile_dkrl_kernel(tc, table, w, w2, offs, out):
                 start=True,
                 stop=True,
             )
-            nc.vector.tensor_reduce(
-                pooled[:, :, first_b:last_b],
-                scores[:].rearrange("f (b p t) -> f p b t", p=POSITIONS, t=WINDOW),
-                mybir.AxisListType.X,
-                mybir.AluOpType.max,
+            pairs = scores[:].rearrange(
+                "f (b p pair t) -> f p b pair t", p=POSITIONS, pair=2, t=2
             )
-            nc.scalar.activation(
-                h1_eighth[:, :, first_b:last_b],
-                pooled[:, :, first_b:last_b],
-                mybir.ActivationFunctionType.Relu,
-                scale=1.0 / POSITIONS,
+            pair_shape = [FILTERS, POSITIONS, PIECE_DESCRIPTIONS, 2]
+            clamped = work.tile(pair_shape, F32, name="clamped")
+            nc.scalar.activation(clamped[:], pairs[:, :, :, 1, :], RELU)
+            best_of_two = work.tile(pair_shape, F32, name="best_of_two")
+            nc.vector.tensor_tensor(best_of_two[:], pairs[:, :, :, 0, :], clamped[:], MAX)
+            nc.vector.tensor_tensor(
+                h1[:, :, first_b:last_b],
+                best_of_two[:, :, :, 0],
+                best_of_two[:, :, :, 1],
+                MAX,
             )
 
-        mean = out_bank.tile([OUT_FEATURES, DESCRIPTIONS], F32, name="mean")
+        total = out_bank.tile([OUT_FEATURES, DESCRIPTIONS], F32, name="total")
         for p in range(POSITIONS):
             nc.tensor.matmul(
-                mean[:],
+                total[:],
                 second_layer[:],
-                h1_eighth[:, p, :],
+                h1[:, p, :],
                 start=(p == 0),
                 stop=(p == POSITIONS - 1),
             )
-        result = held.tile([OUT_FEATURES, DESCRIPTIONS], F32, name="result")
-        nc.vector.tensor_copy(result[:], mean[:])
-        nc.sync.dma_start(out, result[:])
+        mean = held.tile([OUT_FEATURES, DESCRIPTIONS], F32, name="mean")
+        nc.vector.tensor_scalar_mul(mean[:], total[:], 1.0 / POSITIONS)
+        nc.sync.dma_start(out, mean[:])

@@ -1,8 +1,6 @@
 import concourse.mybir as mybir
 
 BF16, F32, U16 = mybir.dt.bfloat16, mybir.dt.float32, mybir.dt.uint16
-MAX = mybir.AluOpType.max
-RELU = mybir.ActivationFunctionType.Relu
 
 FEATURES = 128
 VOCABULARY = 2048
@@ -25,9 +23,8 @@ def tile_dkrl_kernel(tc, table, w, w2, offs, out):
     nc = tc.nc
     with (
         tc.tile_pool(name="held", bufs=1) as held,
-        tc.tile_pool(name="work", bufs=3) as work,
         tc.psum_pool(name="score_banks", bufs=4) as score_banks,
-        tc.psum_pool(name="out_bank", bufs=1) as out_bank,
+        tc.psum_pool(name="out_banks", bufs=2) as out_banks,
     ):
         offsets = held.tile([128, ENTRIES // OFFSETS_IN_A_COLUMN], U16, name="offsets")
         nc.sync.dma_start(offsets[:], offs)
@@ -38,7 +35,8 @@ def tile_dkrl_kernel(tc, table, w, w2, offs, out):
         second_layer = held.tile([FILTERS, OUT_FEATURES], BF16, name="second_layer")
         nc.sync.dma_start(second_layer[:], w2)
 
-        h1 = held.tile([FILTERS, POSITIONS, DESCRIPTIONS], BF16, name="h1")
+        pooled = held.tile([FILTERS, POSITIONS, DESCRIPTIONS], F32, name="pooled")
+        h1_eighth = held.tile([FILTERS, POSITIONS, DESCRIPTIONS], BF16, name="h1_eighth")
 
         for piece in range(PIECES):
             first_column = piece * PIECE // OFFSETS_IN_A_COLUMN
@@ -54,30 +52,30 @@ def tile_dkrl_kernel(tc, table, w, w2, offs, out):
                 start=True,
                 stop=True,
             )
-            pairs = scores[:].rearrange(
-                "f (b p pair t) -> f p b pair t", p=POSITIONS, pair=2, t=2
+            nc.vector.tensor_reduce(
+                pooled[:, :, first_b:last_b],
+                scores[:].rearrange("f (b p t) -> f p b t", p=POSITIONS, t=WINDOW),
+                mybir.AxisListType.X,
+                mybir.AluOpType.max,
             )
-            pair_shape = [FILTERS, POSITIONS, PIECE_DESCRIPTIONS, 2]
-            clamped = work.tile(pair_shape, F32, name="clamped")
-            nc.scalar.activation(clamped[:], pairs[:, :, :, 1, :], RELU)
-            best_of_two = work.tile(pair_shape, F32, name="best_of_two")
-            nc.vector.tensor_tensor(best_of_two[:], pairs[:, :, :, 0, :], clamped[:], MAX)
-            nc.vector.tensor_tensor(
-                h1[:, :, first_b:last_b],
-                best_of_two[:, :, :, 0],
-                best_of_two[:, :, :, 1],
-                MAX,
+            nc.scalar.activation(
+                h1_eighth[:, :, first_b:last_b],
+                pooled[:, :, first_b:last_b],
+                mybir.ActivationFunctionType.Relu,
+                scale=1.0 / POSITIONS,
             )
 
-        total = out_bank.tile([OUT_FEATURES, DESCRIPTIONS], F32, name="total")
-        for p in range(POSITIONS):
-            nc.tensor.matmul(
-                total[:],
-                second_layer[:],
-                h1[:, p, :],
-                start=(p == 0),
-                stop=(p == POSITIONS - 1),
-            )
         mean = held.tile([OUT_FEATURES, DESCRIPTIONS], F32, name="mean")
-        nc.vector.tensor_scalar_mul(mean[:], total[:], 1.0 / POSITIONS)
-        nc.sync.dma_start(out, mean[:])
+        pooled_early = DESCRIPTIONS - PIECE_DESCRIPTIONS
+        for first_b, last_b in ((0, pooled_early), (pooled_early, DESCRIPTIONS)):
+            total = out_banks.tile([OUT_FEATURES, last_b - first_b], F32, name="total")
+            for p in range(POSITIONS):
+                nc.tensor.matmul(
+                    total[:],
+                    second_layer[:],
+                    h1_eighth[:, p, first_b:last_b],
+                    start=(p == 0),
+                    stop=(p == POSITIONS - 1),
+                )
+            nc.vector.tensor_copy(mean[:, first_b:last_b], total[:])
+            nc.sync.dma_start(out[:, first_b:last_b], mean[:, first_b:last_b])

@@ -16,6 +16,9 @@ PIECES = ENTRIES // PIECE
 PIECE_DESCRIPTIONS = PIECE // (POSITIONS * WINDOW)
 OFFSETS_IN_A_COLUMN = 16
 
+TABLE_BLOCKS = 4
+BLOCK_COLUMNS = VOCABULARY // TABLE_BLOCKS
+
 FLOPS = 2 * FEATURES * FILTERS * ENTRIES + 2 * FILTERS * OUT_FEATURES * DESCRIPTIONS
 
 
@@ -29,7 +32,10 @@ def tile_dkrl_kernel(tc, table, w, w2, offs, out):
         offsets = held.tile([128, ENTRIES // OFFSETS_IN_A_COLUMN], U16, name="offsets")
         nc.sync.dma_start(offsets[:], offs)
         words = held.tile([FEATURES, VOCABULARY], BF16, name="words")
-        nc.scalar.dma_start(words[:], table)
+        for block in range(TABLE_BLOCKS):
+            queue = nc.scalar if block % 2 == 0 else nc.sync
+            columns = slice(block * BLOCK_COLUMNS, (block + 1) * BLOCK_COLUMNS)
+            queue.dma_start(words[:, columns], table[:, columns])
         filters = held.tile([FEATURES, FILTERS], BF16, name="filters")
         nc.sync.dma_start(filters[:], w)
         second_layer = held.tile([FILTERS, OUT_FEATURES], BF16, name="second_layer")

@@ -16,9 +16,6 @@ PIECES = ENTRIES // PIECE
 PIECE_DESCRIPTIONS = PIECE // (POSITIONS * WINDOW)
 OFFSETS_IN_A_COLUMN = 16
 
-TABLE_BLOCKS = 4
-BLOCK_COLUMNS = VOCABULARY // TABLE_BLOCKS
-
 FLOPS = 2 * FEATURES * FILTERS * ENTRIES + 2 * FILTERS * OUT_FEATURES * DESCRIPTIONS
 
 
@@ -32,10 +29,7 @@ def tile_dkrl_kernel(tc, table, w, w2, offs, out):
         offsets = held.tile([128, ENTRIES // OFFSETS_IN_A_COLUMN], U16, name="offsets")
         nc.sync.dma_start(offsets[:], offs)
         words = held.tile([FEATURES, VOCABULARY], BF16, name="words")
-        for block in range(TABLE_BLOCKS):
-            queue = nc.scalar if block % 2 == 0 else nc.sync
-            columns = slice(block * BLOCK_COLUMNS, (block + 1) * BLOCK_COLUMNS)
-            queue.dma_start(words[:, columns], table[:, columns])
+        nc.scalar.dma_start(words[:], table)
         filters = held.tile([FEATURES, FILTERS], BF16, name="filters")
         nc.sync.dma_start(filters[:], w)
         second_layer = held.tile([FILTERS, OUT_FEATURES], BF16, name="second_layer")
@@ -64,15 +58,25 @@ def tile_dkrl_kernel(tc, table, w, w2, offs, out):
                 mybir.AxisListType.X,
                 mybir.AluOpType.max,
             )
-            nc.scalar.activation(
-                h1_eighth[:, :, first_b:last_b],
-                pooled[:, :, first_b:last_b],
-                mybir.ActivationFunctionType.Relu,
-                scale=1.0 / POSITIONS,
-            )
+            if piece < PIECES - 1:
+                nc.scalar.activation(
+                    h1_eighth[:, :, first_b:last_b],
+                    pooled[:, :, first_b:last_b],
+                    mybir.ActivationFunctionType.Relu,
+                    scale=1.0 / POSITIONS,
+                )
+            else:
+                nc.vector.tensor_scalar(
+                    h1_eighth[:, :, first_b:last_b],
+                    pooled[:, :, first_b:last_b],
+                    0.0,
+                    1.0 / POSITIONS,
+                    mybir.AluOpType.max,
+                    mybir.AluOpType.mult,
+                )
 
         mean = held.tile([OUT_FEATURES, DESCRIPTIONS], F32, name="mean")
-        pooled_early = DESCRIPTIONS - PIECE_DESCRIPTIONS
+        pooled_early = DESCRIPTIONS - 2 * PIECE_DESCRIPTIONS
         for first_b, last_b in ((0, pooled_early), (pooled_early, DESCRIPTIONS)):
             total = out_banks.tile([OUT_FEATURES, last_b - first_b], F32, name="total")
             for p in range(POSITIONS):

@@ -26,10 +26,12 @@ def tile_dkrl_kernel(tc, table, w, w2, offs, out):
         tc.psum_pool(name="score_banks", bufs=4) as score_banks,
         tc.psum_pool(name="out_banks", bufs=2) as out_banks,
     ):
+        words = held.tile([FEATURES, VOCABULARY], BF16, name="words")
+        half = FEATURES // 2
+        nc.scalar.dma_start(words[:half, :], table[:half, :])
+        nc.sync.dma_start(words[half:, :], table[half:, :])
         offsets = held.tile([128, ENTRIES // OFFSETS_IN_A_COLUMN], U16, name="offsets")
         nc.sync.dma_start(offsets[:], offs)
-        words = held.tile([FEATURES, VOCABULARY], BF16, name="words")
-        nc.scalar.dma_start(words[:], table)
         filters = held.tile([FEATURES, FILTERS], BF16, name="filters")
         nc.sync.dma_start(filters[:], w)
         second_layer = held.tile([FILTERS, OUT_FEATURES], BF16, name="second_layer")
@@ -58,25 +60,15 @@ def tile_dkrl_kernel(tc, table, w, w2, offs, out):
                 mybir.AxisListType.X,
                 mybir.AluOpType.max,
             )
-            if piece < PIECES - 1:
-                nc.scalar.activation(
-                    h1_eighth[:, :, first_b:last_b],
-                    pooled[:, :, first_b:last_b],
-                    mybir.ActivationFunctionType.Relu,
-                    scale=1.0 / POSITIONS,
-                )
-            else:
-                nc.vector.tensor_scalar(
-                    h1_eighth[:, :, first_b:last_b],
-                    pooled[:, :, first_b:last_b],
-                    0.0,
-                    1.0 / POSITIONS,
-                    mybir.AluOpType.max,
-                    mybir.AluOpType.mult,
-                )
+            nc.scalar.activation(
+                h1_eighth[:, :, first_b:last_b],
+                pooled[:, :, first_b:last_b],
+                mybir.ActivationFunctionType.Relu,
+                scale=1.0 / POSITIONS,
+            )
 
         mean = held.tile([OUT_FEATURES, DESCRIPTIONS], F32, name="mean")
-        pooled_early = DESCRIPTIONS - 2 * PIECE_DESCRIPTIONS
+        pooled_early = DESCRIPTIONS - PIECE_DESCRIPTIONS
         for first_b, last_b in ((0, pooled_early), (pooled_early, DESCRIPTIONS)):
             total = out_banks.tile([OUT_FEATURES, last_b - first_b], F32, name="total")
             for p in range(POSITIONS):

@@ -11,7 +11,7 @@ POSITIONS = 8
 WINDOW = 4
 ENTRIES = DESCRIPTIONS * POSITIONS * WINDOW
 
-PIECE = 512
+PIECE = 256
 PIECES = ENTRIES // PIECE
 PIECE_DESCRIPTIONS = PIECE // (POSITIONS * WINDOW)
 OFFSETS_IN_A_COLUMN = 16
@@ -26,12 +26,10 @@ def tile_dkrl_kernel(tc, table, w, w2, offs, out):
         tc.psum_pool(name="score_banks", bufs=4) as score_banks,
         tc.psum_pool(name="out_banks", bufs=2) as out_banks,
     ):
-        words = held.tile([FEATURES, VOCABULARY], BF16, name="words")
-        half = FEATURES // 2
-        nc.scalar.dma_start(words[:half, :], table[:half, :])
-        nc.sync.dma_start(words[half:, :], table[half:, :])
         offsets = held.tile([128, ENTRIES // OFFSETS_IN_A_COLUMN], U16, name="offsets")
         nc.sync.dma_start(offsets[:], offs)
+        words = held.tile([FEATURES, VOCABULARY], BF16, name="words")
+        nc.scalar.dma_start(words[:], table)
         filters = held.tile([FEATURES, FILTERS], BF16, name="filters")
         nc.sync.dma_start(filters[:], w)
         second_layer = held.tile([FILTERS, OUT_FEATURES], BF16, name="second_layer")
@@ -68,7 +66,7 @@ def tile_dkrl_kernel(tc, table, w, w2, offs, out):
             )
 
         mean = held.tile([OUT_FEATURES, DESCRIPTIONS], F32, name="mean")
-        pooled_early = DESCRIPTIONS - PIECE_DESCRIPTIONS
+        pooled_early = DESCRIPTIONS - 2 * PIECE_DESCRIPTIONS
         for first_b, last_b in ((0, pooled_early), (pooled_early, DESCRIPTIONS)):
             total = out_banks.tile([OUT_FEATURES, last_b - first_b], F32, name="total")
             for p in range(POSITIONS):

@@ -26,10 +26,10 @@ def tile_dkrl_kernel(tc, table, w, w2, offs, out):
         tc.psum_pool(name="score_banks", bufs=4) as score_banks,
         tc.psum_pool(name="out_banks", bufs=2) as out_banks,
     ):
+        words = held.tile([FEATURES, VOCABULARY], BF16, name="words")
+        nc.sync.dma_start(words[:], table)
         offsets = held.tile([128, ENTRIES // OFFSETS_IN_A_COLUMN], U16, name="offsets")
         nc.sync.dma_start(offsets[:], offs)
-        words = held.tile([FEATURES, VOCABULARY], BF16, name="words")
-        nc.scalar.dma_start(words[:], table)
         filters = held.tile([FEATURES, FILTERS], BF16, name="filters")
         nc.sync.dma_start(filters[:], w)
         second_layer = held.tile([FILTERS, OUT_FEATURES], BF16, name="second_layer")

@@ -31,9 +31,9 @@ def tile_dkrl_kernel(tc, table, w, w2, offs, out):
         offsets = held.tile([128, ENTRIES // OFFSETS_IN_A_COLUMN], U16, name="offsets")
         nc.sync.dma_start(offsets[:], offs)
         filters = held.tile([FEATURES, FILTERS], BF16, name="filters")
-        nc.sync.dma_start(filters[:], w)
+        nc.scalar.dma_start(filters[:], w)
         second_layer = held.tile([FILTERS, OUT_FEATURES], BF16, name="second_layer")
-        nc.sync.dma_start(second_layer[:], w2)
+        nc.scalar.dma_start(second_layer[:], w2)
 
         pooled = held.tile([FILTERS, POSITIONS, DESCRIPTIONS], F32, name="pooled")
         h1_eighth = held.tile([FILTERS, POSITIONS, DESCRIPTIONS], BF16, name="h1_eighth")

@@ -58,16 +58,28 @@ def tile_dkrl_kernel(tc, table, w, w2, offs, out):
                 mybir.AxisListType.X,
                 mybir.AluOpType.max,
             )
-            nc.scalar.activation(
-                h1_eighth[:, :, first_b:last_b],
-                pooled[:, :, first_b:last_b],
-                mybir.ActivationFunctionType.Relu,
-                scale=1.0 / POSITIONS,
-            )
+            if piece < PIECES - 2:
+                nc.scalar.activation(
+                    h1_eighth[:, :, first_b:last_b],
+                    pooled[:, :, first_b:last_b],
+                    mybir.ActivationFunctionType.Relu,
+                    scale=1.0 / POSITIONS,
+                )
+        clamped_late = slice(DESCRIPTIONS - 2 * PIECE_DESCRIPTIONS, DESCRIPTIONS)
+        nc.vector.tensor_scalar(
+            h1_eighth[:, :, clamped_late],
+            pooled[:, :, clamped_late],
+            0.0,
+            1.0 / POSITIONS,
+            mybir.AluOpType.max,
+            mybir.AluOpType.mult,
+        )
 
-        mean = held.tile([OUT_FEATURES, DESCRIPTIONS], F32, name="mean")
-        pooled_early = DESCRIPTIONS - 2 * PIECE_DESCRIPTIONS
-        for first_b, last_b in ((0, pooled_early), (pooled_early, DESCRIPTIONS)):
+        pooled_early = DESCRIPTIONS - 4 * PIECE_DESCRIPTIONS
+        for first_b, last_b, copy_out, store in (
+            (0, pooled_early, nc.scalar.copy, nc.scalar.dma_start),
+            (pooled_early, DESCRIPTIONS, nc.vector.tensor_copy, nc.sync.dma_start),
+        ):
             total = out_banks.tile([OUT_FEATURES, last_b - first_b], F32, name="total")
             for p in range(POSITIONS):
                 nc.tensor.matmul(
@@ -77,5 +89,6 @@ def tile_dkrl_kernel(tc, table, w, w2, offs, out):
                     start=(p == 0),
                     stop=(p == POSITIONS - 1),
                 )
-            nc.vector.tensor_copy(mean[:, first_b:last_b], total[:])
-            nc.sync.dma_start(out[:, first_b:last_b], mean[:, first_b:last_b])
+            mean = held.tile([OUT_FEATURES, last_b - first_b], F32, name=f"mean_from_{first_b}")
+            copy_out(mean[:], total[:])
+            store(out[:, first_b:last_b], mean[:])

@@ -75,11 +75,9 @@ def tile_dkrl_kernel(tc, table, w, w2, offs, out):
             mybir.AluOpType.mult,
         )
 
+        mean = held.tile([OUT_FEATURES, DESCRIPTIONS], F32, name="mean")
         pooled_early = DESCRIPTIONS - 4 * PIECE_DESCRIPTIONS
-        for first_b, last_b, copy_out, store in (
-            (0, pooled_early, nc.scalar.copy, nc.scalar.dma_start),
-            (pooled_early, DESCRIPTIONS, nc.vector.tensor_copy, nc.sync.dma_start),
-        ):
+        for first_b, last_b in ((0, pooled_early), (pooled_early, DESCRIPTIONS)):
             total = out_banks.tile([OUT_FEATURES, last_b - first_b], F32, name="total")
             for p in range(POSITIONS):
                 nc.tensor.matmul(
@@ -89,6 +87,5 @@ def tile_dkrl_kernel(tc, table, w, w2, offs, out):
                     start=(p == 0),
                     stop=(p == POSITIONS - 1),
                 )
-            mean = held.tile([OUT_FEATURES, last_b - first_b], F32, name=f"mean_from_{first_b}")
-            copy_out(mean[:], total[:])
-            store(out[:, first_b:last_b], mean[:])
+            nc.vector.tensor_copy(mean[:, first_b:last_b], total[:])
+            nc.sync.dma_start(out[:, first_b:last_b], mean[:, first_b:last_b])

@@ -75,9 +75,11 @@ def tile_dkrl_kernel(tc, table, w, w2, offs, out):
             mybir.AluOpType.mult,
         )
 
-        mean = held.tile([OUT_FEATURES, DESCRIPTIONS], F32, name="mean")
         pooled_early = DESCRIPTIONS - 4 * PIECE_DESCRIPTIONS
-        for first_b, last_b in ((0, pooled_early), (pooled_early, DESCRIPTIONS)):
+        for first_b, last_b, copy_out in (
+            (0, pooled_early, nc.scalar.copy),
+            (pooled_early, DESCRIPTIONS, nc.vector.tensor_copy),
+        ):
             total = out_banks.tile([OUT_FEATURES, last_b - first_b], F32, name="total")
             for p in range(POSITIONS):
                 nc.tensor.matmul(
@@ -87,5 +89,6 @@ def tile_dkrl_kernel(tc, table, w, w2, offs, out):
                     start=(p == 0),
                     stop=(p == POSITIONS - 1),
                 )
-            nc.vector.tensor_copy(mean[:, first_b:last_b], total[:])
-            nc.sync.dma_start(out[:, first_b:last_b], mean[:, first_b:last_b])
+            mean = held.tile([OUT_FEATURES, last_b - first_b], F32, name=f"mean_from_{first_b}")
+            copy_out(mean[:], total[:])
+            nc.sync.dma_start(out[:, first_b:last_b], mean[:])

import concourse.mybir as mybir

BF16, F32, U16 = mybir.dt.bfloat16, mybir.dt.float32, mybir.dt.uint16

FEATURES = 128
VOCABULARY = 2048
FILTERS = 128
OUT_FEATURES = 128
DESCRIPTIONS = 128
POSITIONS = 8
WINDOW = 4
ENTRIES = DESCRIPTIONS * POSITIONS * WINDOW

PIECE = 256
PIECES = ENTRIES // PIECE
PIECE_DESCRIPTIONS = PIECE // (POSITIONS * WINDOW)
OFFSETS_IN_A_COLUMN = 16

FLOPS = 2 * FEATURES * FILTERS * ENTRIES + 2 * FILTERS * OUT_FEATURES * DESCRIPTIONS


def tile_dkrl_kernel(tc, table, w, w2, offs, out):
    nc = tc.nc
    with (
        tc.tile_pool(name="held", bufs=1) as held,
        tc.psum_pool(name="score_banks", bufs=4) as score_banks,
        tc.psum_pool(name="out_banks", bufs=2) as out_banks,
    ):
        words = held.tile([FEATURES, VOCABULARY], BF16, name="words")
        nc.sync.dma_start(words[:], table)
        offsets = held.tile([128, ENTRIES // OFFSETS_IN_A_COLUMN], U16, name="offsets")
        nc.sync.dma_start(offsets[:], offs)
        filters = held.tile([FEATURES, FILTERS], BF16, name="filters")
        nc.scalar.dma_start(filters[:], w)
        second_layer = held.tile([FILTERS, OUT_FEATURES], BF16, name="second_layer")
        nc.scalar.dma_start(second_layer[:], w2)

        pooled = held.tile([FILTERS, POSITIONS, DESCRIPTIONS], F32, name="pooled")
        h1_eighth = held.tile([FILTERS, POSITIONS, DESCRIPTIONS], BF16, name="h1_eighth")

        for piece in range(PIECES):
            first_column = piece * PIECE // OFFSETS_IN_A_COLUMN
            last_column = (piece + 1) * PIECE // OFFSETS_IN_A_COLUMN
            first_b = piece * PIECE_DESCRIPTIONS
            last_b = (piece + 1) * PIECE_DESCRIPTIONS

            scores = score_banks.tile([FILTERS, PIECE], F32, name="scores")
            nc.tensor.matmul(
                scores[:],
                filters[:],
                words[:].indirect(offsets[:, first_column:last_column]),
                start=True,
                stop=True,
            )
            nc.vector.tensor_reduce(
                pooled[:, :, first_b:last_b],
                scores[:].rearrange("f (b p t) -> f p b t", p=POSITIONS, t=WINDOW),
                mybir.AxisListType.X,
                mybir.AluOpType.max,
            )
            if piece < PIECES - 2:
                nc.scalar.activation(
                    h1_eighth[:, :, first_b:last_b],
                    pooled[:, :, first_b:last_b],
                    mybir.ActivationFunctionType.Relu,
                    scale=1.0 / POSITIONS,
                )
        clamped_late = slice(DESCRIPTIONS - 2 * PIECE_DESCRIPTIONS, DESCRIPTIONS)
        nc.vector.tensor_scalar(
            h1_eighth[:, :, clamped_late],
            pooled[:, :, clamped_late],
            0.0,
            1.0 / POSITIONS,
            mybir.AluOpType.max,
            mybir.AluOpType.mult,
        )

        pooled_early = DESCRIPTIONS - 4 * PIECE_DESCRIPTIONS
        for first_b, last_b, copy_out in (
            (0, pooled_early, nc.scalar.copy),
            (pooled_early, DESCRIPTIONS, nc.vector.tensor_copy),
        ):
            total = out_banks.tile([OUT_FEATURES, last_b - first_b], F32, name="total")
            for p in range(POSITIONS):
                nc.tensor.matmul(
                    total[:],
                    second_layer[:],
                    h1_eighth[:, p, first_b:last_b],
                    start=(p == 0),
                    stop=(p == POSITIONS - 1),
                )
            mean = held.tile([OUT_FEATURES, last_b - first_b], F32, name=f"mean_from_{first_b}")
            copy_out(mean[:], total[:])
            nc.sync.dma_start(out[:, first_b:last_b], mean[:])
